import numpy as np
import ml_dtypes


def mxq(x, axis, fmt="e4m3"):
    dtype, down = {"e4m3": (ml_dtypes.float8_e4m3fn, 7), "e5m2": (ml_dtypes.float8_e5m2, 14)}[fmt]
    v = np.moveaxis(np.asarray(x, np.float32).astype(ml_dtypes.bfloat16).astype(np.float64), axis, -1)
    blocks = v.reshape(v.shape[:-1] + (-1, 32))
    amax = np.abs(blocks).max(-1, keepdims=True)
    byte = np.maximum(np.where(amax > 0, np.frexp(amax)[1] - 1 + 127, 0) - down, 1)
    scale = np.exp2(byte - 127.0)
    codes = (blocks / scale).astype(np.float32).astype(dtype).astype(np.float64)
    return np.moveaxis((codes * scale).reshape(v.shape), -1, axis)


WIDE = False


def mx_kscale(k):
    if not WIDE:
        return np.ones(k)
    levels = np.array([10, -10, 5, -5, 0])
    a = np.random.permutation(np.resize(levels, k // 512 * 4)).reshape(k // 512, 4)
    idx = np.arange(k)
    return np.exp2(a[idx // 512, idx % 128 // 32])


BF16 = ml_dtypes.bfloat16


def bf(x):
    return np.asarray(x, np.float32).astype(BF16)


def f64(x):
    return np.asarray(x).astype(np.float64)


E2M1 = np.array([0.0, 0.5, 1.0, 1.5, 2.0, 3.0, 4.0, 6.0, -0.0, -0.5, -1.0, -1.5, -2.0, -3.0, -4.0, -6.0])


def pack_weight(w, fmt):
    k, n = w.shape
    w = f64(bf(w)).reshape(k // 32, 32, n)
    amax = np.abs(w).max(1)
    if fmt == "e4m3":
        byte = np.frexp(amax)[1] - 1 + 127 - 7
    else:
        mant, ex = np.frexp(amax / 6.0)
        byte = np.where(mant > 0.5, ex, ex - 1) + 127
    byte = np.clip(np.where(amax > 0, byte, 1), 1, 254)
    scaled = (w * np.exp2(127.0 - byte)[:, None, :]).reshape(k, n).astype(np.float32)
    by_word = np.ascontiguousarray(scaled.reshape(k // 512, 128, 4, n).transpose(0, 1, 3, 2))
    if fmt == "e4m3":
        words = by_word.astype(ml_dtypes.float8_e4m3fn).view(np.uint8)
    else:
        c = by_word.astype(ml_dtypes.float4_e2m1fn).view(np.uint8) & 0xF
        words = c[..., 0::2] | (c[..., 1::2] << 4)
    return np.ascontiguousarray(words), np.ascontiguousarray(byte.astype(np.uint8).reshape(k // 512, 16, n))


def unpack_weight(words, scales, fmt):
    g, p, n, _ = words.shape
    if fmt == "e4m3":
        vals = np.ascontiguousarray(words).view(ml_dtypes.float8_e4m3fn).astype(np.float64)
    else:
        nib = np.empty((g, p, n, 4), np.uint8)
        nib[..., 0::2] = words & 0xF
        nib[..., 1::2] = words >> 4
        vals = E2M1[nib]
    vals = vals * np.repeat(np.exp2(scales.astype(np.float64) - 127.0), 8, axis=1)[..., None]
    return vals.transpose(0, 1, 3, 2).reshape(g * 512, n)

def pack4(w):
    words, scales = pack_weight(w, "e2m1")
    return words.reshape(words.shape[0], 128, -1), scales


def unpack4(words, scales):
    return unpack_weight(words.reshape(words.shape[0], 128, -1, 2), scales, "e2m1")


B, D_IN, D_H = 512, 1024, 1024


def sigmoid(v):
    return 1.0 / (1.0 + np.exp(-v))


def setup_inputs():
    s, t = mx_kscale(D_IN), mx_kscale(D_H)
    fg = np.exp(0.75 * np.random.standard_normal((B, D_H)))
    ig = np.exp(0.75 * np.random.standard_normal((B, D_H)))
    c = fg * np.random.standard_normal((B, D_H)) + ig * np.tanh(0.75 * np.random.standard_normal((B, D_H)))
    n = fg * np.random.uniform(size=(B, D_H)) + ig
    x = bf(np.random.standard_normal((B, D_IN)) * s)
    h_prev = bf(np.random.standard_normal((B, D_H)) * t)
    W_o_words, W_o_scales = pack4(np.random.standard_normal((D_IN, D_H)) * 0.5 / np.sqrt(D_IN) / s[:, None])
    b_o = bf(np.random.standard_normal(D_H) * 0.3)
    U_o_words, U_o_scales = pack4(np.random.standard_normal((D_H, D_H)) * 0.5 / np.sqrt(D_H) / t[:, None])
    return {"x": x,
            "h_prev": h_prev,
            "c": bf(c),
            "n": bf(n),
            "W_o_words": W_o_words,
            "W_o_scales": W_o_scales,
            "b_o": b_o,
            "U_o_words": U_o_words,
            "U_o_scales": U_o_scales}


def reference(x, h_prev, c, n, W_o_words, W_o_scales, b_o, U_o_words, U_o_scales):
    o = sigmoid((mxq(f64(x), 1, "e4m3") @ unpack4(W_o_words, W_o_scales)) + f64(b_o) + (mxq(f64(h_prev), 1, "e4m3") @ unpack4(U_o_words, U_o_scales)))
    return o * (f64(c) / (f64(n) + 1e-6))

@@ -1,0 +1,163 @@
+from contextlib import ExitStack
+
+import concourse.mybir as mybir
+from concourse.masks import make_identity
+
+F32 = mybir.dt.float32
+BF16 = mybir.dt.bfloat16
+I32 = mybir.dt.int32
+U32 = mybir.dt.uint32
+U8 = mybir.dt.uint8
+FP8X4 = mybir.dt.float8_e4m3fn_x4
+FP4X4 = mybir.dt.float4_e2m1fn_x4
+ACT = mybir.ActivationFunctionType
+ALU = mybir.AluOpType
+
+P = 128
+PACK = 4
+K_PASS = P * PACK
+BATCH = 512
+D = 1024
+TILES = BATCH // P
+PASSES = D // K_PASS
+N_BANK = 512
+HALVES = D // N_BANK
+WORDS = K_PASS // 2
+BANKS = 8
+EPS = 1e-6
+
+FLOPS = 2 * BATCH * (D + D) * D
+
+
+def tile_slstmcell_pb_kernel(
+    tc, x, h_prev, c, n, W_o_words, W_o_scales, b_o, U_o_words, U_o_scales, out
+):
+    nc = tc.nc
+    with ExitStack() as stack:
+        keep = stack.enter_context(tc.tile_pool(name="keep", bufs=1))
+        work = stack.enter_context(tc.tile_pool(name="work", bufs=2))
+        psum = stack.enter_context(tc.psum_pool(name="psum", bufs=BANKS))
+        stack.enter_context(tc.manual_schedule())
+
+        def by_tile(dram):
+            return dram.rearrange("(p i) d -> p i d", i=TILES)
+
+        acts_dram = [by_tile(x), by_tile(h_prev)]
+        words_dram = [W_o_words, U_o_words]
+        scales_dram = [W_o_scales, U_o_scales]
+
+        acts = [
+            keep.tile([P, TILES, D], BF16, name="x_sb"),
+            keep.tile([P, TILES, D], BF16, name="h_sb"),
+        ]
+        n_sb = keep.tile([P, TILES, D], BF16)
+        c_sb = keep.tile([P, TILES, D], BF16)
+        w_words = keep.tile([P, 2, PASSES, 2 * D], U8, align_bytes=64)
+        w_scales = keep.tile([P, 2, PASSES, D], U8, align_bytes=64)
+        bias_rows = keep.tile([P, D], BF16)
+        ones = keep.tile([P, P], BF16)
+        eps = keep.tile([P, 1], F32)
+        ident = keep.tile([P, P], F32)
+
+        pairs = [slice(0, 2), slice(2, TILES)]
+
+        def load_scales(o):
+            rows = scales_dram[o].bitcast(I32).rearrange("g (q r) n -> r q g n", r=4)
+            for r in range(4):
+                nc.sync.dma_start(out=w_scales[r:P:32, o, :, :].bitcast(I32), in_=rows[r])
+
+        nc.vector.memset(w_scales[:].rearrange("p o g n -> p (o g n)").bitcast(I32), 0)
+        nc.vector.memset(eps[:], EPS)
+        nc.vector.memset(bias_rows[:], 0.0)
+        nc.vector.memset(ones[:], 1.0)
+        make_identity(nc, ident[:])
+        nc.gpsimd.dma_start(out=bias_rows[0:1, :], in_=b_o.rearrange("(o d) -> o d", o=1))
+
+        nc.sync.dma_start(out=n_sb[:, pairs[0], :], in_=by_tile(n)[:, pairs[0], :])
+        for o in range(2):
+            nc.sync.dma_start(out=acts[o][:, pairs[0], :], in_=acts_dram[o][:, pairs[0], :])
+        nc.sync.dma_start(out=n_sb[:, pairs[1], :], in_=by_tile(n)[:, pairs[1], :])
+        load_scales(0)
+        for o in range(2):
+            nc.sync.dma_start(out=acts[o][:, pairs[1], :], in_=acts_dram[o][:, pairs[1], :])
+        for o in range(2):
+            nc.sync.dma_start(
+                out=w_words[:, o, :, :].bitcast(I32),
+                in_=words_dram[o].bitcast(I32).rearrange("g p b -> p g b"),
+            )
+        load_scales(1)
+        for pair in pairs:
+            nc.sync.dma_start(out=c_sb[:, pair, :], in_=by_tile(c)[:, pair, :])
+
+        ratio = keep.tile([P, TILES, D], F32)
+        for i in range(TILES):
+            nc.scalar.activation(
+                out=ratio[:, i, :], in_=n_sb[:, i, :], func=ACT.Abs_reciprocal_sqrt, bias=eps[:, 0:1], scale=1.0
+            )
+        for i in range(TILES):
+            if i < TILES // 2:
+                nc.gpsimd.tensor_tensor(out=ratio[:, i, :], in0=ratio[:, i, :], in1=ratio[:, i, :], op=ALU.mult)
+            else:
+                nc.scalar.activation(out=ratio[:, i, :], in_=ratio[:, i, :], func=ACT.Square)
+        for i in range(TILES):
+            for j in range(HALVES):
+                cols = slice(j * N_BANK, (j + 1) * N_BANK)
+                nc.gpsimd.tensor_tensor(
+                    out=ratio[:, i, cols], in0=ratio[:, i, cols], in1=c_sb[:, i, cols], op=ALU.mult
+                )
+
+        a_codes = keep.tile([P, TILES, 2, PASSES, P], U32, align_bytes=64)
+        a_scales = keep.tile([P, TILES, 2, PASSES, P], U8, align_bytes=64)
+        for i in range(TILES):
+            grouped = work.tile([P, 2, PASSES, P, 2], F32, align_bytes=64)
+            for o in range(2):
+                words = acts[o][:, i, :].bitcast(F32)
+                flipped = psum.tile([P, PASSES, 2, P], F32, tag="bank")
+                for g in range(PASSES):
+                    for u in range(2):
+                        nc.tensor.transpose(
+                            flipped[:, g, u, :], words[:, g * WORDS + u : (g + 1) * WORDS : 2], ident[:]
+                        )
+                nc.vector.tensor_copy(out=grouped[:, o], in_=flipped[:].rearrange("p g u r -> p g r u"))
+            nc.vector.quantize_mx(
+                out=a_codes[:, i].rearrange("p o g r -> p (o g r)").bitcast(FP8X4),
+                scales=a_scales[:, i].rearrange("p o g r -> p (o g r)"),
+                in_=grouped[:].rearrange("p o g r u -> p (o g r u)").bitcast(BF16),
+            )
+
+        bias_all = keep.tile([P, D], F32)
+        for j in range(HALVES):
+            cols = slice(j * N_BANK, (j + 1) * N_BANK)
+            bias_ps = psum.tile([P, N_BANK], F32, tag="bank")
+            nc.tensor.matmul(out=bias_ps[:], lhsT=ones[:], rhs=bias_rows[:, cols], start=True, stop=True)
+            nc.vector.tensor_copy(out=bias_all[:, cols], in_=bias_ps[:])
+
+        gate = keep.tile([P, TILES, D], F32)
+        result = keep.tile([P, TILES, D], F32)
+        pieces = [(i, j) for i in range(TILES) for j in range(HALVES)]
+
+        def finish(piece):
+            i, j = piece
+            cols = slice(j * N_BANK, (j + 1) * N_BANK)
+            nc.vector.tensor_tensor(out=result[:, i, cols], in0=gate[:, i, cols], in1=ratio[:, i, cols], op=ALU.mult)
+            nc.sync.dma_start(out=by_tile(out)[:, i, cols], in_=result[:, i, cols])
+
+        for number, (i, j) in enumerate(pieces):
+            cols = slice(j * N_BANK, (j + 1) * N_BANK)
+            acc = psum.tile([P, N_BANK], F32, tag="bank")
+            for o in range(2):
+                for g in range(PASSES):
+                    nc.tensor.matmul_mx(
+                        out=acc[:],
+                        lhsT=a_codes[:, i, o, g, :].bitcast(FP8X4),
+                        lhsT_scale=a_scales[:, i, o, g, :],
+                        rhs=w_words[:, o, g, 2 * j * N_BANK : 2 * (j + 1) * N_BANK].bitcast(FP4X4),
+                        rhs_scale=w_scales[:, o, g, cols],
+                        start=(o == 0 and g == 0),
+                        stop=(o == 1 and g == PASSES - 1),
+                    )
+            nc.vector.tensor_tensor(out=gate[:, i, cols], in0=acc[:], in1=bias_all[:, cols], op=ALU.add)
+            nc.scalar.activation(out=gate[:, i, cols], in_=gate[:, i, cols], func=ACT.Sigmoid)
+            if number > 0:
+                finish(pieces[number - 1])
+        finish(pieces[-1])

@@ -24,6 +24,7 @@ N_BANK = 512
 HALVES = D // N_BANK
 WORDS = K_PASS // 2
 BANKS = 8
+AHEAD = 4
 EPS = 1e-6
 
 FLOPS = 2 * BATCH * (D + D) * D
@@ -80,36 +81,27 @@ def tile_slstmcell_pb_kernel(
         load_scales(0)
         for o in range(2):
             nc.sync.dma_start(out=acts[o][:, pairs[1], :], in_=acts_dram[o][:, pairs[1], :])
+        nc.sync.dma_start(out=c_sb[:, pairs[0], :], in_=by_tile(c)[:, pairs[0], :])
         for o in range(2):
             nc.sync.dma_start(
                 out=w_words[:, o, :, :].bitcast(I32),
                 in_=words_dram[o].bitcast(I32).rearrange("g p b -> p g b"),
             )
         load_scales(1)
-        for pair in pairs:
-            nc.sync.dma_start(out=c_sb[:, pair, :], in_=by_tile(c)[:, pair, :])
+        nc.sync.dma_start(out=c_sb[:, pairs[1], :], in_=by_tile(c)[:, pairs[1], :])
 
         ratio = keep.tile([P, TILES, D], F32)
         for i in range(TILES):
             nc.scalar.activation(
                 out=ratio[:, i, :], in_=n_sb[:, i, :], func=ACT.Abs_reciprocal_sqrt, bias=eps[:, 0:1], scale=1.0
             )
-        for i in range(TILES):
-            if i < TILES // 2:
-                nc.gpsimd.tensor_tensor(out=ratio[:, i, :], in0=ratio[:, i, :], in1=ratio[:, i, :], op=ALU.mult)
-            else:
-                nc.scalar.activation(out=ratio[:, i, :], in_=ratio[:, i, :], func=ACT.Square)
-        for i in range(TILES):
-            for j in range(HALVES):
-                cols = slice(j * N_BANK, (j + 1) * N_BANK)
-                nc.gpsimd.tensor_tensor(
-                    out=ratio[:, i, cols], in0=ratio[:, i, cols], in1=c_sb[:, i, cols], op=ALU.mult
-                )
+            nc.scalar.activation(out=ratio[:, i, :], in_=ratio[:, i, :], func=ACT.Square)
 
         a_codes = keep.tile([P, TILES, 2, PASSES, P], U32, align_bytes=64)
         a_scales = keep.tile([P, TILES, 2, PASSES, P], U8, align_bytes=64)
-        for i in range(TILES):
-            grouped = work.tile([P, 2, PASSES, P, 2], F32, align_bytes=64)
+        grouped = keep.tile([P, TILES, 2, PASSES, P, 2], F32, align_bytes=64)
+
+        def transpose_tile(i):
             for o in range(2):
                 words = acts[o][:, i, :].bitcast(F32)
                 flipped = psum.tile([P, PASSES, 2, P], F32, tag="bank")
@@ -118,12 +110,20 @@ def tile_slstmcell_pb_kernel(
                         nc.tensor.transpose(
                             flipped[:, g, u, :], words[:, g * WORDS + u : (g + 1) * WORDS : 2], ident[:]
                         )
-                nc.vector.tensor_copy(out=grouped[:, o], in_=flipped[:].rearrange("p g u r -> p g r u"))
+                nc.vector.tensor_copy(out=grouped[:, i, o], in_=flipped[:].rearrange("p g u r -> p g r u"))
+
+        def quantise_tile(i):
             nc.vector.quantize_mx(
                 out=a_codes[:, i].rearrange("p o g r -> p (o g r)").bitcast(FP8X4),
                 scales=a_scales[:, i].rearrange("p o g r -> p (o g r)"),
-                in_=grouped[:].rearrange("p o g r u -> p (o g r u)").bitcast(BF16),
+                in_=grouped[:, i].rearrange("p o g r u -> p (o g r u)").bitcast(BF16),
             )
+
+        transpose_tile(0)
+        for i in range(1, TILES):
+            transpose_tile(i)
+            quantise_tile(i - 1)
+        quantise_tile(TILES - 1)
 
         bias_all = keep.tile([P, D], F32)
         for j in range(HALVES):
@@ -136,12 +136,19 @@ def tile_slstmcell_pb_kernel(
         result = keep.tile([P, TILES, D], F32)
         pieces = [(i, j) for i in range(TILES) for j in range(HALVES)]
 
+        def times_c(piece):
+            i, j = piece
+            cols = slice(j * N_BANK, (j + 1) * N_BANK)
+            nc.vector.tensor_tensor(out=ratio[:, i, cols], in0=ratio[:, i, cols], in1=c_sb[:, i, cols], op=ALU.mult)
+
         def finish(piece):
             i, j = piece
             cols = slice(j * N_BANK, (j + 1) * N_BANK)
             nc.vector.tensor_tensor(out=result[:, i, cols], in0=gate[:, i, cols], in1=ratio[:, i, cols], op=ALU.mult)
             nc.sync.dma_start(out=by_tile(out)[:, i, cols], in_=result[:, i, cols])
 
+        for piece in pieces[:AHEAD]:
+            times_c(piece)
         for number, (i, j) in enumerate(pieces):
             cols = slice(j * N_BANK, (j + 1) * N_BANK)
             acc = psum.tile([P, N_BANK], F32, tag="bank")
@@ -160,4 +167,6 @@ def tile_slstmcell_pb_kernel(
             nc.scalar.activation(out=gate[:, i, cols], in_=gate[:, i, cols], func=ACT.Sigmoid)
             if number > 0:
                 finish(pieces[number - 1])
+            if number + AHEAD < len(pieces):
+                times_c(pieces[number + AHEAD])
         finish(pieces[-1])

@@ -24,7 +24,6 @@ N_BANK = 512
 HALVES = D // N_BANK
 WORDS = K_PASS // 2
 BANKS = 8
-AHEAD = 4
 EPS = 1e-6
 
 FLOPS = 2 * BATCH * (D + D) * D
@@ -75,20 +74,20 @@ def tile_slstmcell_pb_kernel(
         nc.gpsimd.dma_start(out=bias_rows[0:1, :], in_=b_o.rearrange("(o d) -> o d", o=1))
 
         nc.sync.dma_start(out=n_sb[:, pairs[0], :], in_=by_tile(n)[:, pairs[0], :])
+        nc.sync.dma_start(out=c_sb[:, pairs[0], :], in_=by_tile(c)[:, pairs[0], :])
         for o in range(2):
             nc.sync.dma_start(out=acts[o][:, pairs[0], :], in_=acts_dram[o][:, pairs[0], :])
         nc.sync.dma_start(out=n_sb[:, pairs[1], :], in_=by_tile(n)[:, pairs[1], :])
+        nc.sync.dma_start(out=c_sb[:, pairs[1], :], in_=by_tile(c)[:, pairs[1], :])
         load_scales(0)
         for o in range(2):
             nc.sync.dma_start(out=acts[o][:, pairs[1], :], in_=acts_dram[o][:, pairs[1], :])
-        nc.sync.dma_start(out=c_sb[:, pairs[0], :], in_=by_tile(c)[:, pairs[0], :])
         for o in range(2):
             nc.sync.dma_start(
                 out=w_words[:, o, :, :].bitcast(I32),
                 in_=words_dram[o].bitcast(I32).rearrange("g p b -> p g b"),
             )
         load_scales(1)
-        nc.sync.dma_start(out=c_sb[:, pairs[1], :], in_=by_tile(c)[:, pairs[1], :])
 
         ratio = keep.tile([P, TILES, D], F32)
         for i in range(TILES):
@@ -96,6 +95,11 @@ def tile_slstmcell_pb_kernel(
                 out=ratio[:, i, :], in_=n_sb[:, i, :], func=ACT.Abs_reciprocal_sqrt, bias=eps[:, 0:1], scale=1.0
             )
             nc.scalar.activation(out=ratio[:, i, :], in_=ratio[:, i, :], func=ACT.Square)
+            for j in range(HALVES):
+                cols = slice(j * N_BANK, (j + 1) * N_BANK)
+                nc.gpsimd.tensor_tensor(
+                    out=ratio[:, i, cols], in0=ratio[:, i, cols], in1=c_sb[:, i, cols], op=ALU.mult
+                )
 
         a_codes = keep.tile([P, TILES, 2, PASSES, P], U32, align_bytes=64)
         a_scales = keep.tile([P, TILES, 2, PASSES, P], U8, align_bytes=64)
@@ -136,19 +140,12 @@ def tile_slstmcell_pb_kernel(
         result = keep.tile([P, TILES, D], F32)
         pieces = [(i, j) for i in range(TILES) for j in range(HALVES)]
 
-        def times_c(piece):
-            i, j = piece
-            cols = slice(j * N_BANK, (j + 1) * N_BANK)
-            nc.vector.tensor_tensor(out=ratio[:, i, cols], in0=ratio[:, i, cols], in1=c_sb[:, i, cols], op=ALU.mult)
-
         def finish(piece):
             i, j = piece
             cols = slice(j * N_BANK, (j + 1) * N_BANK)
             nc.vector.tensor_tensor(out=result[:, i, cols], in0=gate[:, i, cols], in1=ratio[:, i, cols], op=ALU.mult)
             nc.sync.dma_start(out=by_tile(out)[:, i, cols], in_=result[:, i, cols])
 
-        for piece in pieces[:AHEAD]:
-            times_c(piece)
         for number, (i, j) in enumerate(pieces):
             cols = slice(j * N_BANK, (j + 1) * N_BANK)
             acc = psum.tile([P, N_BANK], F32, tag="bank")
@@ -167,6 +164,4 @@ def tile_slstmcell_pb_kernel(
             nc.scalar.activation(out=gate[:, i, cols], in_=gate[:, i, cols], func=ACT.Sigmoid)
             if number > 0:
                 finish(pieces[number - 1])
-            if number + AHEAD < len(pieces):
-                times_c(pieces[number + AHEAD])
         finish(pieces[-1])

@@ -24,6 +24,7 @@ N_BANK = 512
 HALVES = D // N_BANK
 WORDS = K_PASS // 2
 BANKS = 8
+LAG = 2
 EPS = 1e-6
 
 FLOPS = 2 * BATCH * (D + D) * D
@@ -162,6 +163,7 @@ def tile_slstmcell_pb_kernel(
                     )
             nc.vector.tensor_tensor(out=gate[:, i, cols], in0=acc[:], in1=bias_all[:, cols], op=ALU.add)
             nc.scalar.activation(out=gate[:, i, cols], in_=gate[:, i, cols], func=ACT.Sigmoid)
-            if number > 0:
-                finish(pieces[number - 1])
-        finish(pieces[-1])
+            if number >= LAG:
+                finish(pieces[number - LAG])
+        for piece in pieces[-LAG:]:
+            finish(piece)

@@ -60,51 +60,72 @@ def tile_slstmcell_pb_kernel(
         eps = keep.tile([P, 1], F32)
         ident = keep.tile([P, P], F32)
 
-        pairs = [slice(0, 2), slice(2, TILES)]
-
-        def load_scales(o):
+        def load_scales(o, which):
             rows = scales_dram[o].bitcast(I32).rearrange("g (q r) n -> r q g n", r=4)
-            for r in range(4):
+            for r in which:
                 nc.sync.dma_start(out=w_scales[r:P:32, o, :, :].bitcast(I32), in_=rows[r])
 
-        nc.vector.memset(w_scales[:].rearrange("p o g n -> p (o g n)").bitcast(I32), 0)
-        nc.vector.memset(eps[:], EPS)
-        nc.vector.memset(bias_rows[:], 0.0)
-        nc.vector.memset(ones[:], 1.0)
-        make_identity(nc, ident[:])
-        nc.gpsimd.dma_start(out=bias_rows[0:1, :], in_=b_o.rearrange("(o d) -> o d", o=1))
+        def load_tile(sbuf, dram, i):
+            nc.sync.dma_start(out=sbuf[:, i, :], in_=by_tile(dram)[:, i, :])
 
-        nc.sync.dma_start(out=n_sb[:, pairs[0], :], in_=by_tile(n)[:, pairs[0], :])
-        nc.sync.dma_start(out=c_sb[:, pairs[0], :], in_=by_tile(c)[:, pairs[0], :])
-        for o in range(2):
-            nc.sync.dma_start(out=acts[o][:, pairs[0], :], in_=acts_dram[o][:, pairs[0], :])
-        nc.sync.dma_start(out=n_sb[:, pairs[1], :], in_=by_tile(n)[:, pairs[1], :])
-        nc.sync.dma_start(out=c_sb[:, pairs[1], :], in_=by_tile(c)[:, pairs[1], :])
-        load_scales(0)
-        for o in range(2):
-            nc.sync.dma_start(out=acts[o][:, pairs[1], :], in_=acts_dram[o][:, pairs[1], :])
-        for o in range(2):
+        def load_acts(i):
+            load_tile(acts[0], x, i)
+            load_tile(acts[1], h_prev, i)
+
+        def load_pair(sbuf, dram):
+            nc.sync.dma_start(out=sbuf[:, 0:2, :], in_=by_tile(dram)[:, 0:2, :])
+
+        def load_words(o):
             nc.sync.dma_start(
                 out=w_words[:, o, :, :].bitcast(I32),
                 in_=words_dram[o].bitcast(I32).rearrange("g p b -> p g b"),
             )
-        load_scales(1)
+
+        nc.vector.memset(bias_rows[:], 0.0)
+        nc.scalar.dma_start(out=bias_rows[0:1, :], in_=b_o.rearrange("(o d) -> o d", o=1))
+        nc.vector.memset(w_scales[:].rearrange("p o g n -> p (o g n)").bitcast(I32), 0)
+        nc.vector.memset(eps[:], EPS)
+        nc.vector.memset(ones[:], 1.0)
+        make_identity(nc, ident[:])
+
+        load_tile(n_sb, n, 0)
+        load_pair(acts[0], x)
+        load_pair(acts[1], h_prev)
+        load_tile(n_sb, n, 1)
+        load_scales(0, [0, 1])
+        load_words(0)
+        load_scales(0, [2, 3])
+        load_scales(1, [0])
+        load_words(1)
+        load_scales(1, [1, 2, 3])
+        for i in (2, 3):
+            load_tile(n_sb, n, i)
+            load_acts(i)
+        load_pair(c_sb, c)
+        nc.sync.dma_start(out=c_sb[:, 2:TILES, :], in_=by_tile(c)[:, 2:TILES, :])
 
         ratio = keep.tile([P, TILES, D], F32)
-        for i in range(TILES):
+        a_codes = keep.tile([P, TILES, 2, PASSES, P], U32, align_bytes=64)
+        a_scales = keep.tile([P, TILES, 2, PASSES, P], U8, align_bytes=64)
+        grouped = keep.tile([P, TILES, 2, PASSES, P, 2], F32, align_bytes=64)
+        bias_all = keep.tile([P, D], BF16)
+        gate = keep.tile([P, TILES, D], F32)
+        result = keep.tile([P, TILES, D], F32)
+        warm = keep.tile([P, 1], F32)
+        banks = {}
+
+        def cols_of(j):
+            return slice(j * N_BANK, (j + 1) * N_BANK)
+
+        def reciprocal(i):
             nc.scalar.activation(
                 out=ratio[:, i, :], in_=n_sb[:, i, :], func=ACT.Abs_reciprocal_sqrt, bias=eps[:, 0:1], scale=1.0
             )
             nc.scalar.activation(out=ratio[:, i, :], in_=ratio[:, i, :], func=ACT.Square)
-            for j in range(HALVES):
-                cols = slice(j * N_BANK, (j + 1) * N_BANK)
-                nc.gpsimd.tensor_tensor(
-                    out=ratio[:, i, cols], in0=ratio[:, i, cols], in1=c_sb[:, i, cols], op=ALU.mult
-                )
 
-        a_codes = keep.tile([P, TILES, 2, PASSES, P], U32, align_bytes=64)
-        a_scales = keep.tile([P, TILES, 2, PASSES, P], U8, align_bytes=64)
-        grouped = keep.tile([P, TILES, 2, PASSES, P, 2], F32, align_bytes=64)
+        def times_c(i, j):
+            cols = cols_of(j)
+            nc.gpsimd.tensor_tensor(out=ratio[:, i, cols], in0=ratio[:, i, cols], in1=c_sb[:, i, cols], op=ALU.mult)
 
         def transpose_tile(i):
             for o in range(2):
@@ -115,7 +136,11 @@ def tile_slstmcell_pb_kernel(
                         nc.tensor.transpose(
                             flipped[:, g, u, :], words[:, g * WORDS + u : (g + 1) * WORDS : 2], ident[:]
                         )
-                nc.vector.tensor_copy(out=grouped[:, i, o], in_=flipped[:].rearrange("p g u r -> p g r u"))
+                banks[("t", i, o)] = flipped
+
+        def copy_tile(i):
+            for o in range(2):
+                nc.vector.tensor_copy(out=grouped[:, i, o], in_=banks[("t", i, o)][:].rearrange("p g u r -> p g r u"))
 
         def quantise_tile(i):
             nc.vector.quantize_mx(
@@ -124,31 +149,7 @@ def tile_slstmcell_pb_kernel(
                 in_=grouped[:, i].rearrange("p o g r u -> p (o g r u)").bitcast(BF16),
             )
 
-        transpose_tile(0)
-        for i in range(1, TILES):
-            transpose_tile(i)
-            quantise_tile(i - 1)
-        quantise_tile(TILES - 1)
-
-        bias_all = keep.tile([P, D], F32)
-        for j in range(HALVES):
-            cols = slice(j * N_BANK, (j + 1) * N_BANK)
-            bias_ps = psum.tile([P, N_BANK], F32, tag="bank")
-            nc.tensor.matmul(out=bias_ps[:], lhsT=ones[:], rhs=bias_rows[:, cols], start=True, stop=True)
-            nc.vector.tensor_copy(out=bias_all[:, cols], in_=bias_ps[:])
-
-        gate = keep.tile([P, TILES, D], F32)
-        result = keep.tile([P, TILES, D], F32)
-        pieces = [(i, j) for i in range(TILES) for j in range(HALVES)]
-
-        def finish(piece):
-            i, j = piece
-            cols = slice(j * N_BANK, (j + 1) * N_BANK)
-            nc.vector.tensor_tensor(out=result[:, i, cols], in0=gate[:, i, cols], in1=ratio[:, i, cols], op=ALU.mult)
-            nc.sync.dma_start(out=by_tile(out)[:, i, cols], in_=result[:, i, cols])
-
-        for number, (i, j) in enumerate(pieces):
-            cols = slice(j * N_BANK, (j + 1) * N_BANK)
+        def multiply(i, j):
             acc = psum.tile([P, N_BANK], F32, tag="bank")
             for o in range(2):
                 for g in range(PASSES):
@@ -157,13 +158,84 @@ def tile_slstmcell_pb_kernel(
                         lhsT=a_codes[:, i, o, g, :].bitcast(FP8X4),
                         lhsT_scale=a_scales[:, i, o, g, :],
                         rhs=w_words[:, o, g, 2 * j * N_BANK : 2 * (j + 1) * N_BANK].bitcast(FP4X4),
-                        rhs_scale=w_scales[:, o, g, cols],
+                        rhs_scale=w_scales[:, o, g, cols_of(j)],
                         start=(o == 0 and g == 0),
                         stop=(o == 1 and g == PASSES - 1),
                     )
-            nc.vector.tensor_tensor(out=gate[:, i, cols], in0=acc[:], in1=bias_all[:, cols], op=ALU.add)
+            banks[("m", i, j)] = acc
+
+        def add_bias(i, j):
+            cols = cols_of(j)
+            nc.vector.tensor_tensor(out=gate[:, i, cols], in0=banks[("m", i, j)][:], in1=bias_all[:, cols], op=ALU.add)
+
+        def sigmoid(i, j):
+            cols = cols_of(j)
             nc.scalar.activation(out=gate[:, i, cols], in_=gate[:, i, cols], func=ACT.Sigmoid)
-            if number >= LAG:
-                finish(pieces[number - LAG])
-        for piece in pieces[-LAG:]:
-            finish(piece)
+
+        def finish(i, j):
+            cols = cols_of(j)
+            nc.vector.tensor_tensor(out=result[:, i, cols], in0=gate[:, i, cols], in1=ratio[:, i, cols], op=ALU.mult)
+            nc.sync.dma_start(out=by_tile(out)[:, i, cols], in_=result[:, i, cols])
+
+        nc.scalar.activation(out=warm[:], in_=eps[:], func=ACT.Abs_reciprocal_sqrt)
+
+        reciprocal(0)
+        transpose_tile(0)
+        bias_ps = psum.tile([P, D], BF16, tag="bank")
+        for j in range(HALVES):
+            nc.tensor.matmul(out=bias_ps[:, cols_of(j)], lhsT=ones[:], rhs=bias_rows[:, cols_of(j)], start=True, stop=True)
+        copy_tile(0)
+        nc.vector.tensor_copy(out=bias_all[:], in_=bias_ps[:])
+        transpose_tile(1)
+        copy_tile(1)
+        quantise_tile(0)
+        quantise_tile(1)
+        reciprocal(1)
+        times_c(0, 0)
+        times_c(0, 1)
+        multiply(0, 0)
+        multiply(1, 0)
+        add_bias(0, 0)
+        transpose_tile(2)
+        add_bias(1, 0)
+        copy_tile(2)
+        reciprocal(2)
+        multiply(0, 1)
+        multiply(1, 1)
+        add_bias(0, 1)
+        quantise_tile(2)
+        times_c(1, 0)
+        times_c(1, 1)
+        transpose_tile(3)
+        add_bias(1, 1)
+        copy_tile(3)
+        reciprocal(3)
+        multiply(2, 0)
+        multiply(2, 1)
+        add_bias(2, 0)
+        quantise_tile(3)
+        times_c(2, 0)
+        times_c(2, 1)
+        sigmoid(0, 0)
+        sigmoid(1, 0)
+        sigmoid(0, 1)
+        finish(0, 0)
+        add_bias(2, 1)
+        multiply(3, 0)
+        multiply(3, 1)
+        times_c(3, 0)
+        times_c(3, 1)
+        sigmoid(1, 1)
+        finish(1, 0)
+        finish(0, 1)
+        add_bias(3, 0)
+        sigmoid(2, 0)
+        sigmoid(2, 1)
+        finish(1, 1)
+        finish(2, 0)
+        add_bias(3, 1)
+        sigmoid(3, 0)
+        finish(2, 1)
+        sigmoid(3, 1)
+        finish(3, 0)
+        finish(3, 1)

@@ -98,10 +98,10 @@ def tile_slstmcell_pb_kernel(
         load_scales(1, [0])
         load_words(1)
         load_scales(1, [1, 2, 3])
+        load_pair(c_sb, c)
         for i in (2, 3):
             load_tile(n_sb, n, i)
             load_acts(i)
-        load_pair(c_sb, c)
         nc.sync.dma_start(out=c_sb[:, 2:TILES, :], in_=by_tile(c)[:, 2:TILES, :])
 
         ratio = keep.tile([P, TILES, D], F32)

@@ -26,6 +26,9 @@ WORDS = K_PASS // 2
 BANKS = 8
 LAG = 2
 EPS = 1e-6
+C_TILES = D // P
+QUAD = N_BANK // P
+TURNED = (2, 3)
 
 FLOPS = 2 * BATCH * (D + D) * D
 
@@ -112,6 +115,8 @@ def tile_slstmcell_pb_kernel(
         gate = keep.tile([P, TILES, D], F32)
         result = keep.tile([P, TILES, D], F32)
         warm = keep.tile([P, 1], F32)
+        bias_cols = keep.tile([P, C_TILES], F32)
+        gate_t = keep.tile([P, len(TURNED), HALVES, QUAD, P], F32)
         banks = {}
 
         def cols_of(j):
@@ -177,6 +182,44 @@ def tile_slstmcell_pb_kernel(
             nc.vector.tensor_tensor(out=result[:, i, cols], in0=gate[:, i, cols], in1=ratio[:, i, cols], op=ALU.mult)
             nc.sync.dma_start(out=by_tile(out)[:, i, cols], in_=result[:, i, cols])
 
+        def multiply_turned(i, j):
+            acc = psum.tile([P, QUAD, P], F32, tag="bank")
+            for q in range(QUAD):
+                m = j * QUAD + q
+                for o in range(2):
+                    for g in range(PASSES):
+                        nc.tensor.matmul_mx(
+                            out=acc[:, q, :],
+                            lhsT=w_words[:, o, g, 2 * m * P : 2 * (m + 1) * P].bitcast(FP4X4),
+                            lhsT_scale=w_scales[:, o, g, m * P : (m + 1) * P],
+                            rhs=a_codes[:, i, o, g, :].bitcast(FP8X4),
+                            rhs_scale=a_scales[:, i, o, g, :],
+                            start=(o == 0 and g == 0),
+                            stop=(o == 1 and g == PASSES - 1),
+                        )
+            banks[("m", i, j)] = acc
+
+        def sigmoid_turned(i, j):
+            for q in range(QUAD):
+                m = j * QUAD + q
+                nc.scalar.activation(
+                    out=gate_t[:, TURNED.index(i), j, q, :], in_=banks[("m", i, j)][:, q, :], func=ACT.Sigmoid,
+                    bias=bias_cols[:, m : m + 1], scale=1.0,
+                )
+
+        def turn_back(i, j):
+            back = psum.tile([P, QUAD, P], F32, tag="bank")
+            for q in range(QUAD):
+                nc.tensor.transpose(back[:, q, :], gate_t[:, TURNED.index(i), j, q, :], ident[:])
+            banks[("b", i, j)] = back
+
+        def finish_turned(i, j):
+            cols = cols_of(j)
+            nc.vector.tensor_tensor(
+                out=result[:, i, cols], in0=banks[("b", i, j)][:].rearrange("p q c -> p (q c)"), in1=ratio[:, i, cols], op=ALU.mult
+            )
+            nc.sync.dma_start(out=by_tile(out)[:, i, cols], in_=result[:, i, cols])
+
         nc.scalar.activation(out=warm[:], in_=eps[:], func=ACT.Abs_reciprocal_sqrt)
 
         reciprocal(0)
@@ -184,8 +227,12 @@ def tile_slstmcell_pb_kernel(
         bias_ps = psum.tile([P, D], BF16, tag="bank")
         for j in range(HALVES):
             nc.tensor.matmul(out=bias_ps[:, cols_of(j)], lhsT=ones[:], rhs=bias_rows[:, cols_of(j)], start=True, stop=True)
+        cols_ps = psum.tile([P, C_TILES, 2], F32, tag="bank")
+        for m in range(C_TILES):
+            nc.tensor.matmul(out=cols_ps[:, m, :], lhsT=bias_rows[:, m * P : (m + 1) * P], rhs=ones[:, 0:2], start=True, stop=True)
         copy_tile(0)
         nc.vector.tensor_copy(out=bias_all[:], in_=bias_ps[:])
+        nc.vector.tensor_copy(out=bias_cols[:], in_=cols_ps[:, :, 0])
         transpose_tile(1)
         copy_tile(1)
         quantise_tile(0)
@@ -210,9 +257,8 @@ def tile_slstmcell_pb_kernel(
         add_bias(1, 1)
         copy_tile(3)
         reciprocal(3)
-        multiply(2, 0)
-        multiply(2, 1)
-        add_bias(2, 0)
+        multiply_turned(2, 0)
+        multiply_turned(2, 1)
         quantise_tile(3)
         times_c(2, 0)
         times_c(2, 1)
@@ -220,22 +266,23 @@ def tile_slstmcell_pb_kernel(
         sigmoid(1, 0)
         sigmoid(0, 1)
         finish(0, 0)
-        add_bias(2, 1)
-        multiply(3, 0)
-        multiply(3, 1)
+        multiply_turned(3, 0)
+        multiply_turned(3, 1)
         times_c(3, 0)
         times_c(3, 1)
         sigmoid(1, 1)
+        sigmoid_turned(2, 0)
+        turn_back(2, 0)
         finish(1, 0)
         finish(0, 1)
-        add_bias(3, 0)
-        sigmoid(2, 0)
-        sigmoid(2, 1)
+        sigmoid_turned(2, 1)
+        turn_back(2, 1)
         finish(1, 1)
-        finish(2, 0)
-        add_bias(3, 1)
-        sigmoid(3, 0)
-        finish(2, 1)
-        sigmoid(3, 1)
-        finish(3, 0)
-        finish(3, 1)
+        finish_turned(2, 0)
+        sigmoid_turned(3, 0)
+        turn_back(3, 0)
+        finish_turned(2, 1)
+        sigmoid_turned(3, 1)
+        turn_back(3, 1)
+        finish_turned(3, 0)
+        finish_turned(3, 1)

@@ -257,8 +257,9 @@ def tile_slstmcell_pb_kernel(
         add_bias(1, 1)
         copy_tile(3)
         reciprocal(3)
-        multiply_turned(2, 0)
+        multiply(2, 0)
         multiply_turned(2, 1)
+        add_bias(2, 0)
         quantise_tile(3)
         times_c(2, 0)
         times_c(2, 1)
@@ -266,23 +267,22 @@ def tile_slstmcell_pb_kernel(
         sigmoid(1, 0)
         sigmoid(0, 1)
         finish(0, 0)
-        multiply_turned(3, 0)
+        multiply(3, 0)
         multiply_turned(3, 1)
         times_c(3, 0)
         times_c(3, 1)
         sigmoid(1, 1)
-        sigmoid_turned(2, 0)
-        turn_back(2, 0)
         finish(1, 0)
         finish(0, 1)
+        add_bias(3, 0)
+        sigmoid(2, 0)
         sigmoid_turned(2, 1)
         turn_back(2, 1)
         finish(1, 1)
-        finish_turned(2, 0)
-        sigmoid_turned(3, 0)
-        turn_back(3, 0)
-        finish_turned(2, 1)
+        finish(2, 0)
+        sigmoid(3, 0)
         sigmoid_turned(3, 1)
         turn_back(3, 1)
-        finish_turned(3, 0)
+        finish_turned(2, 1)
+        finish(3, 0)
         finish_turned(3, 1)

@@ -24,11 +24,11 @@ N_BANK = 512
 HALVES = D // N_BANK
 WORDS = K_PASS // 2
 BANKS = 8
-LAG = 2
 EPS = 1e-6
 C_TILES = D // P
 QUAD = N_BANK // P
 TURNED = (2, 3)
+TURNED_HALF = 1
 
 FLOPS = 2 * BATCH * (D + D) * D
 
@@ -39,14 +39,12 @@ def tile_slstmcell_pb_kernel(
     nc = tc.nc
     with ExitStack() as stack:
         keep = stack.enter_context(tc.tile_pool(name="keep", bufs=1))
-        work = stack.enter_context(tc.tile_pool(name="work", bufs=2))
         psum = stack.enter_context(tc.psum_pool(name="psum", bufs=BANKS))
         stack.enter_context(tc.manual_schedule())
 
         def by_tile(dram):
             return dram.rearrange("(p i) d -> p i d", i=TILES)
 
-        acts_dram = [by_tile(x), by_tile(h_prev)]
         words_dram = [W_o_words, U_o_words]
         scales_dram = [W_o_scales, U_o_scales]
 
@@ -75,8 +73,8 @@ def tile_slstmcell_pb_kernel(
             load_tile(acts[0], x, i)
             load_tile(acts[1], h_prev, i)
 
-        def load_pair(sbuf, dram):
-            nc.sync.dma_start(out=sbuf[:, 0:2, :], in_=by_tile(dram)[:, 0:2, :])
+        def load_pair(sbuf, dram, first):
+            nc.sync.dma_start(out=sbuf[:, first : first + 2, :], in_=by_tile(dram)[:, first : first + 2, :])
 
         def load_words(o):
             nc.sync.dma_start(
@@ -92,8 +90,8 @@ def tile_slstmcell_pb_kernel(
         make_identity(nc, ident[:])
 
         load_tile(n_sb, n, 0)
-        load_pair(acts[0], x)
-        load_pair(acts[1], h_prev)
+        load_pair(acts[0], x, 0)
+        load_pair(acts[1], h_prev, 0)
         load_tile(n_sb, n, 1)
         load_scales(0, [0, 1])
         load_words(0)
@@ -101,11 +99,11 @@ def tile_slstmcell_pb_kernel(
         load_scales(1, [0])
         load_words(1)
         load_scales(1, [1, 2, 3])
-        load_pair(c_sb, c)
+        load_pair(c_sb, c, 0)
         for i in (2, 3):
             load_tile(n_sb, n, i)
             load_acts(i)
-        nc.sync.dma_start(out=c_sb[:, 2:TILES, :], in_=by_tile(c)[:, 2:TILES, :])
+        load_pair(c_sb, c, 2)
 
         ratio = keep.tile([P, TILES, D], F32)
         a_codes = keep.tile([P, TILES, 2, PASSES, P], U32, align_bytes=64)
@@ -115,8 +113,8 @@ def tile_slstmcell_pb_kernel(
         gate = keep.tile([P, TILES, D], F32)
         result = keep.tile([P, TILES, D], F32)
         warm = keep.tile([P, 1], F32)
-        bias_cols = keep.tile([P, C_TILES], F32)
-        gate_t = keep.tile([P, len(TURNED), HALVES, QUAD, P], F32)
+        bias_by_channel = keep.tile([P, C_TILES], F32)
+        gate_t = keep.tile([P, len(TURNED), QUAD, P], F32)
         banks = {}
 
         def cols_of(j):
@@ -182,10 +180,10 @@ def tile_slstmcell_pb_kernel(
             nc.vector.tensor_tensor(out=result[:, i, cols], in0=gate[:, i, cols], in1=ratio[:, i, cols], op=ALU.mult)
             nc.sync.dma_start(out=by_tile(out)[:, i, cols], in_=result[:, i, cols])
 
-        def multiply_turned(i, j):
+        def multiply_turned(i):
             acc = psum.tile([P, QUAD, P], F32, tag="bank")
             for q in range(QUAD):
-                m = j * QUAD + q
+                m = TURNED_HALF * QUAD + q
                 for o in range(2):
                     for g in range(PASSES):
                         nc.tensor.matmul_mx(
@@ -197,28 +195,29 @@ def tile_slstmcell_pb_kernel(
                             start=(o == 0 and g == 0),
                             stop=(o == 1 and g == PASSES - 1),
                         )
-            banks[("m", i, j)] = acc
+            banks[("m", i, TURNED_HALF)] = acc
 
-        def sigmoid_turned(i, j):
+        def sigmoid_turned(i):
             for q in range(QUAD):
-                m = j * QUAD + q
+                m = TURNED_HALF * QUAD + q
                 nc.scalar.activation(
-                    out=gate_t[:, TURNED.index(i), j, q, :], in_=banks[("m", i, j)][:, q, :], func=ACT.Sigmoid,
-                    bias=bias_cols[:, m : m + 1], scale=1.0,
+                    out=gate_t[:, TURNED.index(i), q, :], in_=banks[("m", i, TURNED_HALF)][:, q, :], func=ACT.Sigmoid,
+                    bias=bias_by_channel[:, m : m + 1], scale=1.0,
                 )
 
-        def turn_back(i, j):
+        def turn_back(i):
             back = psum.tile([P, QUAD, P], F32, tag="bank")
             for q in range(QUAD):
-                nc.tensor.transpose(back[:, q, :], gate_t[:, TURNED.index(i), j, q, :], ident[:])
-            banks[("b", i, j)] = back
+                nc.tensor.transpose(back[:, q, :], gate_t[:, TURNED.index(i), q, :], ident[:])
+            banks[("b", i)] = back
 
-        def finish_turned(i, j):
-            cols = cols_of(j)
+        def finish_turned(i):
+            cols = cols_of(TURNED_HALF)
             nc.vector.tensor_tensor(
-                out=result[:, i, cols], in0=banks[("b", i, j)][:].rearrange("p q c -> p (q c)"), in1=ratio[:, i, cols], op=ALU.mult
+                out=result[:, i, cols], in0=banks[("b", i)][:].rearrange("p q c -> p (q c)"), in1=ratio[:, i, cols], op=ALU.mult
             )
             nc.sync.dma_start(out=by_tile(out)[:, i, cols], in_=result[:, i, cols])
+
 
         nc.scalar.activation(out=warm[:], in_=eps[:], func=ACT.Abs_reciprocal_sqrt)
 
@@ -227,12 +226,12 @@ def tile_slstmcell_pb_kernel(
         bias_ps = psum.tile([P, D], BF16, tag="bank")
         for j in range(HALVES):
             nc.tensor.matmul(out=bias_ps[:, cols_of(j)], lhsT=ones[:], rhs=bias_rows[:, cols_of(j)], start=True, stop=True)
-        cols_ps = psum.tile([P, C_TILES, 2], F32, tag="bank")
+        by_channel_ps = psum.tile([P, C_TILES, 2], F32, tag="bank")
         for m in range(C_TILES):
-            nc.tensor.matmul(out=cols_ps[:, m, :], lhsT=bias_rows[:, m * P : (m + 1) * P], rhs=ones[:, 0:2], start=True, stop=True)
+            nc.tensor.matmul(out=by_channel_ps[:, m, :], lhsT=bias_rows[:, m * P : (m + 1) * P], rhs=ones[:, 0:2], start=True, stop=True)
         copy_tile(0)
         nc.vector.tensor_copy(out=bias_all[:], in_=bias_ps[:])
-        nc.vector.tensor_copy(out=bias_cols[:], in_=cols_ps[:, :, 0])
+        nc.vector.tensor_copy(out=bias_by_channel[:], in_=by_channel_ps[:, :, 0])
         transpose_tile(1)
         copy_tile(1)
         quantise_tile(0)
@@ -240,6 +239,7 @@ def tile_slstmcell_pb_kernel(
         reciprocal(1)
         times_c(0, 0)
         times_c(0, 1)
+
         multiply(0, 0)
         multiply(1, 0)
         add_bias(0, 0)
@@ -257,8 +257,9 @@ def tile_slstmcell_pb_kernel(
         add_bias(1, 1)
         copy_tile(3)
         reciprocal(3)
+
         multiply(2, 0)
-        multiply_turned(2, 1)
+        multiply_turned(2)
         add_bias(2, 0)
         quantise_tile(3)
         times_c(2, 0)
@@ -268,7 +269,7 @@ def tile_slstmcell_pb_kernel(
         sigmoid(0, 1)
         finish(0, 0)
         multiply(3, 0)
-        multiply_turned(3, 1)
+        multiply_turned(3)
         times_c(3, 0)
         times_c(3, 1)
         sigmoid(1, 1)
@@ -276,13 +277,13 @@ def tile_slstmcell_pb_kernel(
         finish(0, 1)
         add_bias(3, 0)
         sigmoid(2, 0)
-        sigmoid_turned(2, 1)
-        turn_back(2, 1)
+        sigmoid_turned(2)
+        turn_back(2)
         finish(1, 1)
         finish(2, 0)
         sigmoid(3, 0)
-        sigmoid_turned(3, 1)
-        turn_back(3, 1)
-        finish_turned(2, 1)
+        sigmoid_turned(3)
+        turn_back(3)
+        finish_turned(2)
         finish(3, 0)
-        finish_turned(3, 1)
+        finish_turned(3)

@@ -54,8 +54,14 @@ def tile_slstmcell_pb_kernel(
         ]
         n_sb = keep.tile([P, TILES, D], BF16)
         c_sb = keep.tile([P, TILES, D], BF16)
-        w_words = keep.tile([P, 2, PASSES, 2 * D], U8, align_bytes=64)
-        w_scales = keep.tile([P, 2, PASSES, D], U8, align_bytes=64)
+        w_words = [
+            keep.tile([P, PASSES, 2 * D], U8, align_bytes=64, name="w_words"),
+            keep.tile([P, PASSES, 2 * D], U8, align_bytes=64, name="u_words"),
+        ]
+        w_scales = [
+            keep.tile([P, PASSES, D], U8, align_bytes=64, name="w_scales"),
+            keep.tile([P, PASSES, D], U8, align_bytes=64, name="u_scales"),
+        ]
         bias_rows = keep.tile([P, D], BF16)
         ones = keep.tile([P, P], BF16)
         eps = keep.tile([P, 1], F32)
@@ -64,7 +70,7 @@ def tile_slstmcell_pb_kernel(
         def load_scales(o, which):
             rows = scales_dram[o].bitcast(I32).rearrange("g (q r) n -> r q g n", r=4)
             for r in which:
-                nc.sync.dma_start(out=w_scales[r:P:32, o, :, :].bitcast(I32), in_=rows[r])
+                nc.sync.dma_start(out=w_scales[o][r:P:32, :, :].bitcast(I32), in_=rows[r])
 
         def load_tile(sbuf, dram, i):
             nc.sync.dma_start(out=sbuf[:, i, :], in_=by_tile(dram)[:, i, :])
@@ -78,41 +84,49 @@ def tile_slstmcell_pb_kernel(
 
         def load_words(o):
             nc.sync.dma_start(
-                out=w_words[:, o, :, :].bitcast(I32),
+                out=w_words[o][:].bitcast(I32),
                 in_=words_dram[o].bitcast(I32).rearrange("g p b -> p g b"),
             )
 
-        nc.vector.memset(bias_rows[:], 0.0)
-        nc.scalar.dma_start(out=bias_rows[0:1, :], in_=b_o.rearrange("(o d) -> o d", o=1))
-        nc.vector.memset(w_scales[:].rearrange("p o g n -> p (o g n)").bitcast(I32), 0)
+        warm = keep.tile([P, 1], F32)
         nc.vector.memset(eps[:], EPS)
+        nc.scalar.activation(out=warm[:], in_=eps[:], func=ACT.Abs_reciprocal_sqrt)
+        nc.vector.memset(bias_rows[:].bitcast(I32), 0)
+        for o in range(2):
+            nc.vector.memset(w_scales[o][:].rearrange("p g n -> p (g n)").bitcast(I32), 0)
         nc.vector.memset(ones[:], 1.0)
         make_identity(nc, ident[:])
 
-        load_tile(n_sb, n, 0)
         load_pair(acts[0], x, 0)
+        nc.sync.dma_start(out=bias_rows[0:1, :], in_=b_o.rearrange("(o d) -> o d", o=1))
+        load_tile(n_sb, n, 0)
         load_pair(acts[1], h_prev, 0)
-        load_tile(n_sb, n, 1)
         load_scales(0, [0, 1])
         load_words(0)
         load_scales(0, [2, 3])
-        load_scales(1, [0])
+        load_tile(n_sb, n, 1)
+        load_tile(n_sb, n, 2)
+        load_scales(1, [0, 1])
         load_words(1)
-        load_scales(1, [1, 2, 3])
+        load_scales(1, [2, 3])
+        load_acts(2)
         load_pair(c_sb, c, 0)
-        for i in (2, 3):
-            load_tile(n_sb, n, i)
-            load_acts(i)
+        load_tile(n_sb, n, 3)
+        load_acts(3)
         load_pair(c_sb, c, 2)
 
+        UNITS = 2 * TILES
+
+        def unit(i, o):
+            return 2 * o + i if i < 2 else 2 * i + o
+
         ratio = keep.tile([P, TILES, D], F32)
-        a_codes = keep.tile([P, TILES, 2, PASSES, P], U32, align_bytes=64)
-        a_scales = keep.tile([P, TILES, 2, PASSES, P], U8, align_bytes=64)
-        grouped = keep.tile([P, TILES, 2, PASSES, P, 2], F32, align_bytes=64)
+        a_codes = keep.tile([P, UNITS, PASSES, P], U32, align_bytes=64)
+        a_scales = keep.tile([P, UNITS, PASSES, P], U8, align_bytes=64)
+        grouped = keep.tile([P, UNITS, PASSES, P, 2], F32, align_bytes=64)
         bias_all = keep.tile([P, D], BF16)
         gate = keep.tile([P, TILES, D], F32)
         result = keep.tile([P, TILES, D], F32)
-        warm = keep.tile([P, 1], F32)
         bias_by_channel = keep.tile([P, C_TILES], F32)
         gate_t = keep.tile([P, len(TURNED), QUAD, P], F32)
         banks = {}
@@ -130,42 +144,38 @@ def tile_slstmcell_pb_kernel(
             cols = cols_of(j)
             nc.gpsimd.tensor_tensor(out=ratio[:, i, cols], in0=ratio[:, i, cols], in1=c_sb[:, i, cols], op=ALU.mult)
 
-        def transpose_tile(i):
-            for o in range(2):
-                words = acts[o][:, i, :].bitcast(F32)
-                flipped = psum.tile([P, PASSES, 2, P], F32, tag="bank")
-                for g in range(PASSES):
-                    for u in range(2):
-                        nc.tensor.transpose(
-                            flipped[:, g, u, :], words[:, g * WORDS + u : (g + 1) * WORDS : 2], ident[:]
-                        )
-                banks[("t", i, o)] = flipped
+        def transpose_unit(i, o):
+            words = acts[o][:, i, :].bitcast(F32)
+            flipped = psum.tile([P, PASSES, 2, P], F32, tag="bank")
+            for g in range(PASSES):
+                for u in range(2):
+                    nc.tensor.transpose(flipped[:, g, u, :], words[:, g * WORDS + u : (g + 1) * WORDS : 2], ident[:])
+            banks[("t", i, o)] = flipped
 
-        def copy_tile(i):
-            for o in range(2):
-                nc.vector.tensor_copy(out=grouped[:, i, o], in_=banks[("t", i, o)][:].rearrange("p g u r -> p g r u"))
+        def copy_unit(i, o):
+            nc.vector.tensor_copy(out=grouped[:, unit(i, o)], in_=banks[("t", i, o)][:].rearrange("p g u r -> p g r u"))
 
-        def quantise_tile(i):
+        def quantise_units(first):
             nc.vector.quantize_mx(
-                out=a_codes[:, i].rearrange("p o g r -> p (o g r)").bitcast(FP8X4),
-                scales=a_scales[:, i].rearrange("p o g r -> p (o g r)"),
-                in_=grouped[:, i].rearrange("p o g r u -> p (o g r u)").bitcast(BF16),
+                out=a_codes[:, first : first + 2].rearrange("p a g r -> p (a g r)").bitcast(FP8X4),
+                scales=a_scales[:, first : first + 2].rearrange("p a g r -> p (a g r)"),
+                in_=grouped[:, first : first + 2].rearrange("p a g r u -> p (a g r u)").bitcast(BF16),
             )
 
-        def multiply(i, j):
-            acc = psum.tile([P, N_BANK], F32, tag="bank")
-            for o in range(2):
-                for g in range(PASSES):
-                    nc.tensor.matmul_mx(
-                        out=acc[:],
-                        lhsT=a_codes[:, i, o, g, :].bitcast(FP8X4),
-                        lhsT_scale=a_scales[:, i, o, g, :],
-                        rhs=w_words[:, o, g, 2 * j * N_BANK : 2 * (j + 1) * N_BANK].bitcast(FP4X4),
-                        rhs_scale=w_scales[:, o, g, cols_of(j)],
-                        start=(o == 0 and g == 0),
-                        stop=(o == 1 and g == PASSES - 1),
-                    )
-            banks[("m", i, j)] = acc
+        def open_bank(i, j):
+            banks[("m", i, j)] = psum.tile([P, N_BANK], F32, tag="bank", name="acc")
+
+        def multiply(i, j, o):
+            for g in range(PASSES):
+                nc.tensor.matmul_mx(
+                    out=banks[("m", i, j)][:],
+                    lhsT=a_codes[:, unit(i, o), g, :].bitcast(FP8X4),
+                    lhsT_scale=a_scales[:, unit(i, o), g, :],
+                    rhs=w_words[o][:, g, 2 * j * N_BANK : 2 * (j + 1) * N_BANK].bitcast(FP4X4),
+                    rhs_scale=w_scales[o][:, g, cols_of(j)],
+                    start=(o == 0 and g == 0),
+                    stop=(o == 1 and g == PASSES - 1),
+                )
 
         def add_bias(i, j):
             cols = cols_of(j)
@@ -188,10 +198,10 @@ def tile_slstmcell_pb_kernel(
                     for g in range(PASSES):
                         nc.tensor.matmul_mx(
                             out=acc[:, q, :],
-                            lhsT=w_words[:, o, g, 2 * m * P : 2 * (m + 1) * P].bitcast(FP4X4),
-                            lhsT_scale=w_scales[:, o, g, m * P : (m + 1) * P],
-                            rhs=a_codes[:, i, o, g, :].bitcast(FP8X4),
-                            rhs_scale=a_scales[:, i, o, g, :],
+                            lhsT=w_words[o][:, g, 2 * m * P : 2 * (m + 1) * P].bitcast(FP4X4),
+                            lhsT_scale=w_scales[o][:, g, m * P : (m + 1) * P],
+                            rhs=a_codes[:, unit(i, o), g, :].bitcast(FP8X4),
+                            rhs_scale=a_scales[:, unit(i, o), g, :],
                             start=(o == 0 and g == 0),
                             stop=(o == 1 and g == PASSES - 1),
                         )
@@ -218,63 +228,76 @@ def tile_slstmcell_pb_kernel(
             )
             nc.sync.dma_start(out=by_tile(out)[:, i, cols], in_=result[:, i, cols])
 
-
-        nc.scalar.activation(out=warm[:], in_=eps[:], func=ACT.Abs_reciprocal_sqrt)
-
         reciprocal(0)
-        transpose_tile(0)
+        transpose_unit(0, 0)
+        transpose_unit(1, 0)
         bias_ps = psum.tile([P, D], BF16, tag="bank")
         for j in range(HALVES):
             nc.tensor.matmul(out=bias_ps[:, cols_of(j)], lhsT=ones[:], rhs=bias_rows[:, cols_of(j)], start=True, stop=True)
         by_channel_ps = psum.tile([P, C_TILES, 2], F32, tag="bank")
         for m in range(C_TILES):
             nc.tensor.matmul(out=by_channel_ps[:, m, :], lhsT=bias_rows[:, m * P : (m + 1) * P], rhs=ones[:, 0:2], start=True, stop=True)
-        copy_tile(0)
+        copy_unit(0, 0)
+        copy_unit(1, 0)
         nc.vector.tensor_copy(out=bias_all[:], in_=bias_ps[:])
+        quantise_units(unit(0, 0))
+        transpose_unit(0, 1)
+        transpose_unit(1, 1)
+        copy_unit(0, 1)
+        copy_unit(1, 1)
         nc.vector.tensor_copy(out=bias_by_channel[:], in_=by_channel_ps[:, :, 0])
-        transpose_tile(1)
-        copy_tile(1)
-        quantise_tile(0)
-        quantise_tile(1)
+        quantise_units(unit(0, 1))
         reciprocal(1)
+        reciprocal(2)
+
+        for i in (0, 1):
+            for j in range(HALVES):
+                open_bank(i, j)
+                multiply(i, j, 0)
+        multiply(0, 0, 1)
+        multiply(0, 1, 1)
+        add_bias(0, 0)
+        add_bias(0, 1)
+        transpose_unit(2, 0)
+        transpose_unit(2, 1)
+        copy_unit(2, 0)
+        copy_unit(2, 1)
+        multiply(1, 0, 1)
+        multiply(1, 1, 1)
+        add_bias(1, 0)
+        quantise_units(unit(2, 0))
+        add_bias(1, 1)
         times_c(0, 0)
         times_c(0, 1)
-
-        multiply(0, 0)
-        multiply(1, 0)
-        add_bias(0, 0)
-        transpose_tile(2)
-        add_bias(1, 0)
-        copy_tile(2)
-        reciprocal(2)
-        multiply(0, 1)
-        multiply(1, 1)
-        add_bias(0, 1)
-        quantise_tile(2)
         times_c(1, 0)
         times_c(1, 1)
-        transpose_tile(3)
-        add_bias(1, 1)
-        copy_tile(3)
         reciprocal(3)
+        transpose_unit(3, 0)
+        transpose_unit(3, 1)
+        copy_unit(3, 0)
+        copy_unit(3, 1)
 
-        multiply(2, 0)
+        open_bank(2, 0)
+        multiply(2, 0, 0)
+        multiply(2, 0, 1)
         multiply_turned(2)
         add_bias(2, 0)
-        quantise_tile(3)
+        quantise_units(unit(3, 0))
         times_c(2, 0)
         times_c(2, 1)
         sigmoid(0, 0)
-        sigmoid(1, 0)
         sigmoid(0, 1)
+        sigmoid(1, 0)
         finish(0, 0)
-        multiply(3, 0)
+        open_bank(3, 0)
+        multiply(3, 0, 0)
+        multiply(3, 0, 1)
         multiply_turned(3)
         times_c(3, 0)
         times_c(3, 1)
         sigmoid(1, 1)
-        finish(1, 0)
         finish(0, 1)
+        finish(1, 0)
         add_bias(3, 0)
         sigmoid(2, 0)
         sigmoid_turned(2)

@@ -105,15 +105,16 @@ def tile_slstmcell_pb_kernel(
         load_words(0)
         load_scales(0, [2, 3])
         load_tile(n_sb, n, 1)
+        load_pair(c_sb, c, 0)
         load_tile(n_sb, n, 2)
         load_scales(1, [0, 1])
         load_words(1)
         load_scales(1, [2, 3])
         load_acts(2)
-        load_pair(c_sb, c, 0)
         load_tile(n_sb, n, 3)
+        load_tile(c_sb, c, 2)
         load_acts(3)
-        load_pair(c_sb, c, 2)
+        load_tile(c_sb, c, 3)
 
         UNITS = 2 * TILES
 

@@ -141,9 +141,9 @@ def tile_slstmcell_pb_kernel(
             )
             nc.scalar.activation(out=ratio[:, i, :], in_=ratio[:, i, :], func=ACT.Square)
 
-        def times_c(i, j):
+        def times_c(i, j, engine):
             cols = cols_of(j)
-            nc.gpsimd.tensor_tensor(out=ratio[:, i, cols], in0=ratio[:, i, cols], in1=c_sb[:, i, cols], op=ALU.mult)
+            engine.tensor_tensor(out=ratio[:, i, cols], in0=ratio[:, i, cols], in1=c_sb[:, i, cols], op=ALU.mult)
 
         def transpose_unit(i, o):
             words = acts[o][:, i, :].bitcast(F32)
@@ -268,10 +268,10 @@ def tile_slstmcell_pb_kernel(
         add_bias(1, 0)
         quantise_units(unit(2, 0))
         add_bias(1, 1)
-        times_c(0, 0)
-        times_c(0, 1)
-        times_c(1, 0)
-        times_c(1, 1)
+        times_c(0, 0, nc.gpsimd)
+        times_c(0, 1, nc.gpsimd)
+        times_c(1, 0, nc.gpsimd)
+        times_c(1, 1, nc.gpsimd)
         reciprocal(3)
         transpose_unit(3, 0)
         transpose_unit(3, 1)
@@ -284,18 +284,18 @@ def tile_slstmcell_pb_kernel(
         multiply_turned(2)
         add_bias(2, 0)
         quantise_units(unit(3, 0))
-        times_c(2, 0)
-        times_c(2, 1)
+        times_c(2, 0, nc.gpsimd)
+        times_c(2, 1, nc.gpsimd)
         sigmoid(0, 0)
         sigmoid(0, 1)
         sigmoid(1, 0)
+        times_c(3, 0, nc.vector)
+        times_c(3, 1, nc.vector)
         finish(0, 0)
         open_bank(3, 0)
         multiply(3, 0, 0)
         multiply(3, 0, 1)
         multiply_turned(3)
-        times_c(3, 0)
-        times_c(3, 1)
         sigmoid(1, 1)
         finish(0, 1)
         finish(1, 0)

@@ -97,21 +97,22 @@ def tile_slstmcell_pb_kernel(
         nc.vector.memset(ones[:], 1.0)
         make_identity(nc, ident[:])
 
+        load_tile(n_sb, n, 0)
         load_pair(acts[0], x, 0)
         nc.sync.dma_start(out=bias_rows[0:1, :], in_=b_o.rearrange("(o d) -> o d", o=1))
-        load_tile(n_sb, n, 0)
+        load_tile(n_sb, n, 1)
         load_pair(acts[1], h_prev, 0)
+        load_tile(c_sb, c, 0)
         load_scales(0, [0, 1])
         load_words(0)
         load_scales(0, [2, 3])
-        load_tile(n_sb, n, 1)
-        load_pair(c_sb, c, 0)
         load_tile(n_sb, n, 2)
+        load_tile(c_sb, c, 1)
         load_scales(1, [0, 1])
         load_words(1)
         load_scales(1, [2, 3])
-        load_acts(2)
         load_tile(n_sb, n, 3)
+        load_acts(2)
         load_tile(c_sb, c, 2)
         load_acts(3)
         load_tile(c_sb, c, 3)
@@ -155,6 +156,18 @@ def tile_slstmcell_pb_kernel(
 
         def copy_unit(i, o):
             nc.vector.tensor_copy(out=grouped[:, unit(i, o)], in_=banks[("t", i, o)][:].rearrange("p g u r -> p g r u"))
+
+        def copy_unit_scalar(i, o):
+            nc.scalar.copy(out=grouped[:, unit(i, o)], in_=banks[("t", i, o)][:].rearrange("p g u r -> p g r u"))
+
+        seen_codes = keep.tile([P, 2], U32)
+        seen_ratio = keep.tile([P, 1], F32)
+
+        def gpsimd_waits_for_codes(first, k):
+            nc.gpsimd.tensor_copy(out=seen_codes[:, k : k + 1], in_=a_codes[:, first + 1, PASSES - 1, P - 1 : P])
+
+        def gpsimd_waits_for_product(i, j):
+            nc.gpsimd.tensor_copy(out=seen_ratio[:, 0:1], in_=ratio[:, i, (j + 1) * N_BANK - 1 : (j + 1) * N_BANK])
 
         def quantise_units(first):
             nc.vector.quantize_mx(
@@ -242,6 +255,8 @@ def tile_slstmcell_pb_kernel(
         copy_unit(1, 0)
         nc.vector.tensor_copy(out=bias_all[:], in_=bias_ps[:])
         quantise_units(unit(0, 0))
+        gpsimd_waits_for_codes(unit(0, 0), 0)
+        times_c(0, 0, nc.gpsimd)
         transpose_unit(0, 1)
         transpose_unit(1, 1)
         copy_unit(0, 1)
@@ -250,6 +265,11 @@ def tile_slstmcell_pb_kernel(
         quantise_units(unit(0, 1))
         reciprocal(1)
         reciprocal(2)
+        times_c(0, 1, nc.vector)
+        times_c(1, 0, nc.vector)
+        gpsimd_waits_for_product(1, 0)
+        times_c(1, 1, nc.gpsimd)
+        times_c(2, 0, nc.gpsimd)
 
         for i in (0, 1):
             for j in range(HALVES):
@@ -262,44 +282,41 @@ def tile_slstmcell_pb_kernel(
         transpose_unit(2, 0)
         transpose_unit(2, 1)
         copy_unit(2, 0)
-        copy_unit(2, 1)
+        reciprocal(3)
+        copy_unit_scalar(2, 1)
         multiply(1, 0, 1)
         multiply(1, 1, 1)
         add_bias(1, 0)
         quantise_units(unit(2, 0))
+        gpsimd_waits_for_codes(unit(2, 0), 1)
+        times_c(2, 1, nc.gpsimd)
         add_bias(1, 1)
-        times_c(0, 0, nc.gpsimd)
-        times_c(0, 1, nc.gpsimd)
-        times_c(1, 0, nc.gpsimd)
-        times_c(1, 1, nc.gpsimd)
-        reciprocal(3)
         transpose_unit(3, 0)
         transpose_unit(3, 1)
+        nc.scalar.activation(out=warm[:], in_=eps[:], func=ACT.Sigmoid)
         copy_unit(3, 0)
-        copy_unit(3, 1)
+        copy_unit_scalar(3, 1)
 
         open_bank(2, 0)
         multiply(2, 0, 0)
         multiply(2, 0, 1)
         multiply_turned(2)
-        add_bias(2, 0)
         quantise_units(unit(3, 0))
-        times_c(2, 0, nc.gpsimd)
-        times_c(2, 1, nc.gpsimd)
+        add_bias(2, 0)
+        times_c(3, 0, nc.vector)
+        times_c(3, 1, nc.vector)
         sigmoid(0, 0)
         sigmoid(0, 1)
         sigmoid(1, 0)
-        times_c(3, 0, nc.vector)
-        times_c(3, 1, nc.vector)
         finish(0, 0)
         open_bank(3, 0)
         multiply(3, 0, 0)
         multiply(3, 0, 1)
         multiply_turned(3)
+        add_bias(3, 0)
         sigmoid(1, 1)
         finish(0, 1)
         finish(1, 0)
-        add_bias(3, 0)
         sigmoid(2, 0)
         sigmoid_turned(2)
         turn_back(2)

@@ -130,7 +130,7 @@ def tile_slstmcell_pb_kernel(
         gate = keep.tile([P, TILES, D], F32)
         result = keep.tile([P, TILES, D], F32)
         bias_by_channel = keep.tile([P, C_TILES], F32)
-        gate_t = keep.tile([P, len(TURNED), QUAD, P], F32)
+        gate_t = keep.tile([P, len(TURNED), HALVES, QUAD, P], F32)
         banks = {}
 
         def cols_of(j):
@@ -204,10 +204,10 @@ def tile_slstmcell_pb_kernel(
             nc.vector.tensor_tensor(out=result[:, i, cols], in0=gate[:, i, cols], in1=ratio[:, i, cols], op=ALU.mult)
             nc.sync.dma_start(out=by_tile(out)[:, i, cols], in_=result[:, i, cols])
 
-        def multiply_turned(i):
+        def multiply_turned(i, j):
             acc = psum.tile([P, QUAD, P], F32, tag="bank")
             for q in range(QUAD):
-                m = TURNED_HALF * QUAD + q
+                m = j * QUAD + q
                 for o in range(2):
                     for g in range(PASSES):
                         nc.tensor.matmul_mx(
@@ -219,26 +219,26 @@ def tile_slstmcell_pb_kernel(
                             start=(o == 0 and g == 0),
                             stop=(o == 1 and g == PASSES - 1),
                         )
-            banks[("m", i, TURNED_HALF)] = acc
+            banks[("m", i, j)] = acc
 
-        def sigmoid_turned(i):
+        def sigmoid_turned(i, j):
             for q in range(QUAD):
-                m = TURNED_HALF * QUAD + q
+                m = j * QUAD + q
                 nc.scalar.activation(
-                    out=gate_t[:, TURNED.index(i), q, :], in_=banks[("m", i, TURNED_HALF)][:, q, :], func=ACT.Sigmoid,
+                    out=gate_t[:, TURNED.index(i), j, q, :], in_=banks[("m", i, j)][:, q, :], func=ACT.Sigmoid,
                     bias=bias_by_channel[:, m : m + 1], scale=1.0,
                 )
 
-        def turn_back(i):
+        def turn_back(i, j):
             back = psum.tile([P, QUAD, P], F32, tag="bank")
             for q in range(QUAD):
-                nc.tensor.transpose(back[:, q, :], gate_t[:, TURNED.index(i), q, :], ident[:])
-            banks[("b", i)] = back
+                nc.tensor.transpose(back[:, q, :], gate_t[:, TURNED.index(i), j, q, :], ident[:])
+            banks[("b", i, j)] = back
 
-        def finish_turned(i):
-            cols = cols_of(TURNED_HALF)
+        def finish_turned(i, j):
+            cols = cols_of(j)
             nc.vector.tensor_tensor(
-                out=result[:, i, cols], in0=banks[("b", i)][:].rearrange("p q c -> p (q c)"), in1=ratio[:, i, cols], op=ALU.mult
+                out=result[:, i, cols], in0=banks[("b", i, j)][:].rearrange("p q c -> p (q c)"), in1=ratio[:, i, cols], op=ALU.mult
             )
             nc.sync.dma_start(out=by_tile(out)[:, i, cols], in_=result[:, i, cols])
 
@@ -297,34 +297,30 @@ def tile_slstmcell_pb_kernel(
         copy_unit(3, 0)
         copy_unit_scalar(3, 1)
 
-        open_bank(2, 0)
-        multiply(2, 0, 0)
-        multiply(2, 0, 1)
-        multiply_turned(2)
+        multiply_turned(2, 0)
+        multiply_turned(2, 1)
         quantise_units(unit(3, 0))
-        add_bias(2, 0)
         times_c(3, 0, nc.vector)
         times_c(3, 1, nc.vector)
         sigmoid(0, 0)
         sigmoid(0, 1)
         sigmoid(1, 0)
-        finish(0, 0)
-        open_bank(3, 0)
-        multiply(3, 0, 0)
-        multiply(3, 0, 1)
-        multiply_turned(3)
-        add_bias(3, 0)
         sigmoid(1, 1)
+        finish(0, 0)
         finish(0, 1)
         finish(1, 0)
-        sigmoid(2, 0)
-        sigmoid_turned(2)
-        turn_back(2)
         finish(1, 1)
-        finish(2, 0)
-        sigmoid(3, 0)
-        sigmoid_turned(3)
-        turn_back(3)
-        finish_turned(2)
-        finish(3, 0)
-        finish_turned(3)
+        multiply_turned(3, 0)
+        multiply_turned(3, 1)
+        sigmoid_turned(2, 0)
+        sigmoid_turned(2, 1)
+        sigmoid_turned(3, 0)
+        sigmoid_turned(3, 1)
+        turn_back(2, 0)
+        turn_back(2, 1)
+        turn_back(3, 0)
+        turn_back(3, 1)
+        finish_turned(2, 0)
+        finish_turned(2, 1)
+        finish_turned(3, 0)
+        finish_turned(3, 1)

from contextlib import ExitStack

import concourse.mybir as mybir
from concourse.masks import make_identity

F32 = mybir.dt.float32
BF16 = mybir.dt.bfloat16
I32 = mybir.dt.int32
U32 = mybir.dt.uint32
U8 = mybir.dt.uint8
FP8X4 = mybir.dt.float8_e4m3fn_x4
FP4X4 = mybir.dt.float4_e2m1fn_x4
ACT = mybir.ActivationFunctionType
ALU = mybir.AluOpType

P = 128
PACK = 4
K_PASS = P * PACK
BATCH = 512
D = 1024
TILES = BATCH // P
PASSES = D // K_PASS
N_BANK = 512
HALVES = D // N_BANK
WORDS = K_PASS // 2
BANKS = 8
EPS = 1e-6
C_TILES = D // P
QUAD = N_BANK // P
TURNED = (2, 3)
TURNED_HALF = 1

FLOPS = 2 * BATCH * (D + D) * D


def tile_slstmcell_pb_kernel(
    tc, x, h_prev, c, n, W_o_words, W_o_scales, b_o, U_o_words, U_o_scales, out
):
    nc = tc.nc
    with ExitStack() as stack:
        keep = stack.enter_context(tc.tile_pool(name="keep", bufs=1))
        psum = stack.enter_context(tc.psum_pool(name="psum", bufs=BANKS))
        stack.enter_context(tc.manual_schedule())

        def by_tile(dram):
            return dram.rearrange("(p i) d -> p i d", i=TILES)

        words_dram = [W_o_words, U_o_words]
        scales_dram = [W_o_scales, U_o_scales]

        acts = [
            keep.tile([P, TILES, D], BF16, name="x_sb"),
            keep.tile([P, TILES, D], BF16, name="h_sb"),
        ]
        n_sb = keep.tile([P, TILES, D], BF16)
        c_sb = keep.tile([P, TILES, D], BF16)
        w_words = [
            keep.tile([P, PASSES, 2 * D], U8, align_bytes=64, name="w_words"),
            keep.tile([P, PASSES, 2 * D], U8, align_bytes=64, name="u_words"),
        ]
        w_scales = [
            keep.tile([P, PASSES, D], U8, align_bytes=64, name="w_scales"),
            keep.tile([P, PASSES, D], U8, align_bytes=64, name="u_scales"),
        ]
        bias_rows = keep.tile([P, D], BF16)
        ones = keep.tile([P, P], BF16)
        eps = keep.tile([P, 1], F32)
        ident = keep.tile([P, P], F32)

        def load_scales(o, which):
            rows = scales_dram[o].bitcast(I32).rearrange("g (q r) n -> r q g n", r=4)
            for r in which:
                nc.sync.dma_start(out=w_scales[o][r:P:32, :, :].bitcast(I32), in_=rows[r])

        def load_tile(sbuf, dram, i):
            nc.sync.dma_start(out=sbuf[:, i, :], in_=by_tile(dram)[:, i, :])

        def load_acts(i):
            load_tile(acts[0], x, i)
            load_tile(acts[1], h_prev, i)

        def load_pair(sbuf, dram, first):
            nc.sync.dma_start(out=sbuf[:, first : first + 2, :], in_=by_tile(dram)[:, first : first + 2, :])

        def load_words(o):
            nc.sync.dma_start(
                out=w_words[o][:].bitcast(I32),
                in_=words_dram[o].bitcast(I32).rearrange("g p b -> p g b"),
            )

        warm = keep.tile([P, 1], F32)
        nc.vector.memset(eps[:], EPS)
        nc.scalar.activation(out=warm[:], in_=eps[:], func=ACT.Abs_reciprocal_sqrt)
        nc.vector.memset(bias_rows[:].bitcast(I32), 0)
        for o in range(2):
            nc.vector.memset(w_scales[o][:].rearrange("p g n -> p (g n)").bitcast(I32), 0)
        nc.vector.memset(ones[:], 1.0)
        make_identity(nc, ident[:])

        load_tile(n_sb, n, 0)
        load_pair(acts[0], x, 0)
        nc.sync.dma_start(out=bias_rows[0:1, :], in_=b_o.rearrange("(o d) -> o d", o=1))
        load_tile(n_sb, n, 1)
        load_pair(acts[1], h_prev, 0)
        load_tile(c_sb, c, 0)
        load_scales(0, [0, 1])
        load_words(0)
        load_scales(0, [2, 3])
        load_tile(n_sb, n, 2)
        load_tile(c_sb, c, 1)
        load_scales(1, [0, 1])
        load_words(1)
        load_scales(1, [2, 3])
        load_tile(n_sb, n, 3)
        load_acts(2)
        load_tile(c_sb, c, 2)
        load_acts(3)
        load_tile(c_sb, c, 3)

        UNITS = 2 * TILES

        def unit(i, o):
            return 2 * o + i if i < 2 else 2 * i + o

        ratio = keep.tile([P, TILES, D], F32)
        a_codes = keep.tile([P, UNITS, PASSES, P], U32, align_bytes=64)
        a_scales = keep.tile([P, UNITS, PASSES, P], U8, align_bytes=64)
        grouped = keep.tile([P, UNITS, PASSES, P, 2], F32, align_bytes=64)
        bias_all = keep.tile([P, D], BF16)
        gate = keep.tile([P, TILES, D], F32)
        result = keep.tile([P, TILES, D], F32)
        bias_by_channel = keep.tile([P, C_TILES], F32)
        gate_t = keep.tile([P, len(TURNED), HALVES, QUAD, P], F32)
        banks = {}

        def cols_of(j):
            return slice(j * N_BANK, (j + 1) * N_BANK)

        def reciprocal(i):
            nc.scalar.activation(
                out=ratio[:, i, :], in_=n_sb[:, i, :], func=ACT.Abs_reciprocal_sqrt, bias=eps[:, 0:1], scale=1.0
            )
            nc.scalar.activation(out=ratio[:, i, :], in_=ratio[:, i, :], func=ACT.Square)

        def times_c(i, j, engine):
            cols = cols_of(j)
            engine.tensor_tensor(out=ratio[:, i, cols], in0=ratio[:, i, cols], in1=c_sb[:, i, cols], op=ALU.mult)

        def transpose_unit(i, o):
            words = acts[o][:, i, :].bitcast(F32)
            flipped = psum.tile([P, PASSES, 2, P], F32, tag="bank")
            for g in range(PASSES):
                for u in range(2):
                    nc.tensor.transpose(flipped[:, g, u, :], words[:, g * WORDS + u : (g + 1) * WORDS : 2], ident[:])
            banks[("t", i, o)] = flipped

        def copy_unit(i, o):
            nc.vector.tensor_copy(out=grouped[:, unit(i, o)], in_=banks[("t", i, o)][:].rearrange("p g u r -> p g r u"))

        def copy_unit_scalar(i, o):
            nc.scalar.copy(out=grouped[:, unit(i, o)], in_=banks[("t", i, o)][:].rearrange("p g u r -> p g r u"))

        seen_codes = keep.tile([P, 2], U32)
        seen_ratio = keep.tile([P, 1], F32)

        def gpsimd_waits_for_codes(first, k):
            nc.gpsimd.tensor_copy(out=seen_codes[:, k : k + 1], in_=a_codes[:, first + 1, PASSES - 1, P - 1 : P])

        def gpsimd_waits_for_product(i, j):
            nc.gpsimd.tensor_copy(out=seen_ratio[:, 0:1], in_=ratio[:, i, (j + 1) * N_BANK - 1 : (j + 1) * N_BANK])

        def quantise_units(first):
            nc.vector.quantize_mx(
                out=a_codes[:, first : first + 2].rearrange("p a g r -> p (a g r)").bitcast(FP8X4),
                scales=a_scales[:, first : first + 2].rearrange("p a g r -> p (a g r)"),
                in_=grouped[:, first : first + 2].rearrange("p a g r u -> p (a g r u)").bitcast(BF16),
            )

        def open_bank(i, j):
            banks[("m", i, j)] = psum.tile([P, N_BANK], F32, tag="bank", name="acc")

        def multiply(i, j, o):
            for g in range(PASSES):
                nc.tensor.matmul_mx(
                    out=banks[("m", i, j)][:],
                    lhsT=a_codes[:, unit(i, o), g, :].bitcast(FP8X4),
                    lhsT_scale=a_scales[:, unit(i, o), g, :],
                    rhs=w_words[o][:, g, 2 * j * N_BANK : 2 * (j + 1) * N_BANK].bitcast(FP4X4),
                    rhs_scale=w_scales[o][:, g, cols_of(j)],
                    start=(o == 0 and g == 0),
                    stop=(o == 1 and g == PASSES - 1),
                )

        def add_bias(i, j):
            cols = cols_of(j)
            nc.vector.tensor_tensor(out=gate[:, i, cols], in0=banks[("m", i, j)][:], in1=bias_all[:, cols], op=ALU.add)

        def sigmoid(i, j):
            cols = cols_of(j)
            nc.scalar.activation(out=gate[:, i, cols], in_=gate[:, i, cols], func=ACT.Sigmoid)

        def finish(i, j):
            cols = cols_of(j)
            nc.vector.tensor_tensor(out=result[:, i, cols], in0=gate[:, i, cols], in1=ratio[:, i, cols], op=ALU.mult)
            nc.sync.dma_start(out=by_tile(out)[:, i, cols], in_=result[:, i, cols])

        def multiply_turned(i, j):
            acc = psum.tile([P, QUAD, P], F32, tag="bank")
            for q in range(QUAD):
                m = j * QUAD + q
                for o in range(2):
                    for g in range(PASSES):
                        nc.tensor.matmul_mx(
                            out=acc[:, q, :],
                            lhsT=w_words[o][:, g, 2 * m * P : 2 * (m + 1) * P].bitcast(FP4X4),
                            lhsT_scale=w_scales[o][:, g, m * P : (m + 1) * P],
                            rhs=a_codes[:, unit(i, o), g, :].bitcast(FP8X4),
                            rhs_scale=a_scales[:, unit(i, o), g, :],
                            start=(o == 0 and g == 0),
                            stop=(o == 1 and g == PASSES - 1),
                        )
            banks[("m", i, j)] = acc

        def sigmoid_turned(i, j):
            for q in range(QUAD):
                m = j * QUAD + q
                nc.scalar.activation(
                    out=gate_t[:, TURNED.index(i), j, q, :], in_=banks[("m", i, j)][:, q, :], func=ACT.Sigmoid,
                    bias=bias_by_channel[:, m : m + 1], scale=1.0,
                )

        def turn_back(i, j):
            back = psum.tile([P, QUAD, P], F32, tag="bank")
            for q in range(QUAD):
                nc.tensor.transpose(back[:, q, :], gate_t[:, TURNED.index(i), j, q, :], ident[:])
            banks[("b", i, j)] = back

        def finish_turned(i, j):
            cols = cols_of(j)
            nc.vector.tensor_tensor(
                out=result[:, i, cols], in0=banks[("b", i, j)][:].rearrange("p q c -> p (q c)"), in1=ratio[:, i, cols], op=ALU.mult
            )
            nc.sync.dma_start(out=by_tile(out)[:, i, cols], in_=result[:, i, cols])

        reciprocal(0)
        transpose_unit(0, 0)
        transpose_unit(1, 0)
        bias_ps = psum.tile([P, D], BF16, tag="bank")
        for j in range(HALVES):
            nc.tensor.matmul(out=bias_ps[:, cols_of(j)], lhsT=ones[:], rhs=bias_rows[:, cols_of(j)], start=True, stop=True)
        by_channel_ps = psum.tile([P, C_TILES, 2], F32, tag="bank")
        for m in range(C_TILES):
            nc.tensor.matmul(out=by_channel_ps[:, m, :], lhsT=bias_rows[:, m * P : (m + 1) * P], rhs=ones[:, 0:2], start=True, stop=True)
        copy_unit(0, 0)
        copy_unit(1, 0)
        nc.vector.tensor_copy(out=bias_all[:], in_=bias_ps[:])
        quantise_units(unit(0, 0))
        gpsimd_waits_for_codes(unit(0, 0), 0)
        times_c(0, 0, nc.gpsimd)
        transpose_unit(0, 1)
        transpose_unit(1, 1)
        copy_unit(0, 1)
        copy_unit(1, 1)
        nc.vector.tensor_copy(out=bias_by_channel[:], in_=by_channel_ps[:, :, 0])
        quantise_units(unit(0, 1))
        reciprocal(1)
        reciprocal(2)
        times_c(0, 1, nc.vector)
        times_c(1, 0, nc.vector)
        gpsimd_waits_for_product(1, 0)
        times_c(1, 1, nc.gpsimd)
        times_c(2, 0, nc.gpsimd)

        for i in (0, 1):
            for j in range(HALVES):
                open_bank(i, j)
                multiply(i, j, 0)
        multiply(0, 0, 1)
        multiply(0, 1, 1)
        add_bias(0, 0)
        add_bias(0, 1)
        transpose_unit(2, 0)
        transpose_unit(2, 1)
        copy_unit(2, 0)
        reciprocal(3)
        copy_unit_scalar(2, 1)
        multiply(1, 0, 1)
        multiply(1, 1, 1)
        add_bias(1, 0)
        quantise_units(unit(2, 0))
        gpsimd_waits_for_codes(unit(2, 0), 1)
        times_c(2, 1, nc.gpsimd)
        add_bias(1, 1)
        transpose_unit(3, 0)
        transpose_unit(3, 1)
        nc.scalar.activation(out=warm[:], in_=eps[:], func=ACT.Sigmoid)
        copy_unit(3, 0)
        copy_unit_scalar(3, 1)

        multiply_turned(2, 0)
        multiply_turned(2, 1)
        quantise_units(unit(3, 0))
        times_c(3, 0, nc.vector)
        times_c(3, 1, nc.vector)
        sigmoid(0, 0)
        sigmoid(0, 1)
        sigmoid(1, 0)
        sigmoid(1, 1)
        finish(0, 0)
        finish(0, 1)
        finish(1, 0)
        finish(1, 1)
        multiply_turned(3, 0)
        multiply_turned(3, 1)
        sigmoid_turned(2, 0)
        sigmoid_turned(2, 1)
        sigmoid_turned(3, 0)
        sigmoid_turned(3, 1)
        turn_back(2, 0)
        turn_back(2, 1)
        turn_back(3, 0)
        turn_back(3, 1)
        finish_turned(2, 0)
        finish_turned(2, 1)
        finish_turned(3, 0)
        finish_turned(3, 1)
